import numpy as np
import ml_dtypes


def mxq(x, axis, fmt="e4m3"):
    dtype, down = {"e4m3": (ml_dtypes.float8_e4m3fn, 7), "e5m2": (ml_dtypes.float8_e5m2, 14)}[fmt]
    v = np.moveaxis(np.asarray(x, np.float32).astype(ml_dtypes.bfloat16).astype(np.float64), axis, -1)
    blocks = v.reshape(v.shape[:-1] + (-1, 32))
    amax = np.abs(blocks).max(-1, keepdims=True)
    byte = np.maximum(np.where(amax > 0, np.frexp(amax)[1] - 1 + 127, 0) - down, 1)
    scale = np.exp2(byte - 127.0)
    codes = (blocks / scale).astype(np.float32).astype(dtype).astype(np.float64)
    return np.moveaxis((codes * scale).reshape(v.shape), -1, axis)


WIDE = False


def mx_kscale(k):
    if not WIDE:
        return np.ones(k)
    levels = np.array([10, -10, 5, -5, 0])
    if k % 512:
        return np.exp2(np.random.permutation(np.resize(levels, k // 32))).repeat(32)
    a = np.empty((k // 512, 16))
    for p in range(k // 512):
        a[p, :8] = np.random.permutation(np.resize(levels, 8))
        for g in range(8):
            far = levels[np.abs(levels - a[p, g]) >= 10]
            a[p, g + 8] = far[np.random.randint(len(far))]
    return np.exp2(a.ravel()).repeat(32)


BF16 = ml_dtypes.bfloat16


def bf(x):
    return np.asarray(x, np.float32).astype(BF16)


def f64(x):
    return np.asarray(x).astype(np.float64)


N, V, M0, M1, M2 = 1024, 128, 128, 64, 32
MUL = [(M0, 1), (M1, 3), (M2, 5)]
DX = sum(m * d for m, d in MUL)
J0 = M0 * M0
J = sum(m * m for m, d in MUL)


def dt_block(xs, gs, alpha):
    n, mul, d = xs.shape
    t = np.zeros((n, mul, mul))
    for m in range(d):
        t = t + xs[:, :, None, m] * gs[:, None, :, m]
    return (t * alpha).reshape(n, mul * mul)


def setup_inputs():
    s = mx_kscale(N)[:, None]
    k = mx_kscale(J)
    fu, off = [], 0
    for mul, d in MUL:
        fu.append(k[off:off + mul * mul:mul])
        off += mul * mul
    fx = np.concatenate([np.repeat(f, d) for f, (mul, d) in zip(fu, MUL)])
    ws = 8.0 / np.sqrt(V)
    x = bf(np.random.standard_normal((N, DX)) * fx)
    z = bf(np.random.standard_normal((N, V)) * s)
    w0 = bf(np.random.standard_normal((M0, V, M0)) * ws / fu[0][:, None, None])
    w1 = bf(np.random.standard_normal((M1, V, M1)) * ws / fu[1][:, None, None])
    w2 = bf(np.random.standard_normal((M2, V, M2)) * ws / fu[2][:, None, None])
    g = bf(np.random.standard_normal((N, DX)) * np.exp2(np.random.randint(-6, 1, (N, 1))) * 8.0 / s)
    return {"x": x, "z": z, "w0": w0, "w1": w1, "w2": w2, "grad_out": g}


def reference(x, z, w0, w1, w2, grad_out):
    x = f64(x)
    g = f64(grad_out)
    dts, wjs, off = [], [], 0
    for (mul, d), w in zip(MUL, (w0, w1, w2)):
        xs = x[:, off:off + mul * d].reshape(-1, mul, d)
        gs = g[:, off:off + mul * d].reshape(-1, mul, d)
        dts.append(dt_block(xs, gs, 1.0 / np.sqrt(mul * V)))
        wjs.append(f64(w).transpose(1, 0, 2).reshape(V, mul * mul))
        off += mul * d
    dt = np.concatenate(dts, axis=1)
    wj = np.concatenate(wjs, axis=1)
    dz = mxq(dt, 1, "e5m2") @ mxq(wj, 1, "e4m3").T
    dw = mxq(f64(z), 0, "e4m3").T @ mxq(dts[0], 0, "e5m2")
    return dz, np.ascontiguousarray(dw.reshape(V, M0, M0).transpose(1, 0, 2))

@@ -1,0 +1,510 @@
+import math
+from contextlib import ExitStack
+
+import concourse.mybir as mybir
+from concourse.masks import make_identity
+
+F32 = mybir.dt.float32
+BF16 = mybir.dt.bfloat16
+U32 = mybir.dt.uint32
+U8 = mybir.dt.uint8
+E4 = mybir.dt.float8_e4m3fn_x4
+E5 = mybir.dt.float8_e5m2_x4
+MULT = mybir.AluOpType.mult
+ADD = mybir.AluOpType.add
+COPY = mybir.ActivationFunctionType.Copy
+
+P = 128
+N, V = 1024, 128
+FLOPS = 2 * N * V * (128 * 128 + 64 * 64 + 32 * 32) + 2 * N * V * 128 * 128
+ALPHA0 = 1.0 / 128
+ALPHA1 = 1.0 / math.sqrt(64 * 128)
+ALPHA2 = 1.0 / 64
+ROW = 144
+STEPS = 32
+
+
+def tile_selfconnectionintro_v_kernel(tc, x, z, w0, w1, w2, grad_out, out_0, out_1):
+    nc = tc.nc
+    with ExitStack() as ctx:
+        keep = ctx.enter_context(tc.tile_pool(name="keep", bufs=1))
+        ring = ctx.enter_context(tc.tile_pool(name="ring", bufs=2))
+        accp = ctx.enter_context(tc.psum_pool(name="accp", bufs=1))
+        psum = ctx.enter_context(tc.psum_pool(name="psum", bufs=6))
+
+        def big(shape, dtype, name):
+            t = ring.tile(shape, dtype, name=name, tag="big", bufs=4, align_bytes=64)
+            return t
+
+        def bank(name):
+            t = psum.tile([P, 512], F32, name=name, tag="bank")
+            return t
+
+        x_v = x.rearrange("(g p j) w -> g p j w", g=2, j=4)
+        g_v = grad_out.rearrange("(g p j) w -> g p j w", g=2, j=4)
+        park_x = out_0[0:512, :]
+        park_m = out_1[92:128].rearrange("u v c -> (u v c)")
+
+        g0 = keep.tile([P, 2, 4, 128], BF16, name="g0")
+        x0 = keep.tile([P, 2, 4, 128], BF16, name="x0")
+        for g in range(2):
+            nc.sync.dma_start(out=g0[:, g], in_=g_v[g, :, :, 0:128])
+            nc.sync.dma_start(out=x0[:, g], in_=x_v[g, :, :, 0:128])
+        zin = keep.tile([P, 2, 4, 128], BF16, name="zin")
+        nc.sync.dma_start(out=zin[:].rearrange("p g j v -> p g (j v)"), in_=z.rearrange("(g p j) v -> p g (j v)", g=2, j=4))
+        xr = ring.tile([P, 2, 4, 352], BF16, name="xr", tag="fm", align_bytes=64)
+        gr = ring.tile([P, 2, 4, 352], BF16, name="gr", tag="fm", align_bytes=64)
+        for g in range(2):
+            nc.sync.dma_start(out=xr[:, g], in_=x_v[g, :, :, 128:480])
+            nc.sync.dma_start(out=gr[:, g], in_=g_v[g, :, :, 128:480])
+
+        ident = keep.tile([P, P], F32, name="ident")
+        make_identity(nc, ident[:])
+        pm = []
+        for g in range(2):
+            t = ring.tile([P, 4, 8, ROW], BF16, name="pm", tag="lhs")
+            nc.gpsimd.memset(t[:].rearrange("p j r w -> p (j r w)").bitcast(F32), 0.0)
+            pm.append(t)
+        dts = []
+        for i in range(3):
+            t = keep.tile([P, 2, 256], BF16, name="dstage%d" % i)
+            nc.gpsimd.memset(t[:, :, 224:256], 0.0)
+            dts.append(t)
+
+        w_raw, w_bank, w_t, w_codes, w_scales = {}, {}, {}, {}, {}
+
+        def w_passes(grp):
+            return 3 if grp == 10 else 4
+
+        def w_load(grp):
+            if grp < 8:
+                t = ring.tile([P, 16, 128], BF16, name="wraw", tag="wraw")
+                nc.sync.dma_start(out=t[:], in_=w0[16 * grp : 16 * grp + 16].rearrange("u v c -> v u c"))
+                w_raw[grp] = t[:].rearrange("p u c -> p (u c)").bitcast(F32)
+            elif grp < 10:
+                t = ring.tile([P, 4, 512], BF16, name="wraw", tag="wraw")
+                nc.gpsimd.memset(t[:, :, 448:512], 0.0)
+                ug0 = 4 * (grp - 8)
+                for a in range(5):
+                    nc.sync.dma_start(out=t[:, :, 64 * a : 64 * a + 64], in_=w1[8 * a + ug0 : 8 * a + ug0 + 4].rearrange("u v c -> v u c"))
+                for a in range(4):
+                    nc.sync.dma_start(out=t[:, :, 320 + 32 * a : 352 + 32 * a], in_=w2[8 * a + ug0 : 8 * a + ug0 + 4].rearrange("u v c -> v u c"))
+                w_raw[grp] = t[:].rearrange("p u c -> p (u c)").bitcast(F32)
+            else:
+                t = ring.tile([P, 24, 64], BF16, name="wraw", tag="wraw")
+                nc.sync.dma_start(out=t[:], in_=w1[40:64].rearrange("u v c -> v u c"))
+                w_raw[grp] = t[:].rearrange("p u c -> p (u c)").bitcast(F32)
+
+        def w_tr(grp, half):
+            b = bank("wbank")
+            for i in range(min(2, w_passes(grp) - 2 * half)):
+                s = 2 * half + i
+                for h in range(2):
+                    nc.tensor.transpose(b[:, 256 * i + 128 * h : 256 * i + 128 * h + 128], w_raw[grp][:, 256 * s + h : 256 * s + 256 : 2], ident[:])
+            w_bank[grp, half] = b
+
+        def w_cp(grp, half):
+            if half == 0:
+                w_t[grp] = ring.tile([P, 4, 128, 2], F32, name="wt", tag="wt", align_bytes=64)
+            n = min(2, w_passes(grp) - 2 * half)
+            nc.scalar.copy(out=w_t[grp][:, 2 * half : 2 * half + n], in_=w_bank[grp, half][:, 0 : 256 * n].rearrange("p (s h v) -> p s v h", h=2, v=128))
+
+        def w_q(grp):
+            n = w_passes(grp)
+            w_codes[grp] = keep.tile([P, 128 * n], U32, name="wc%d" % grp, align_bytes=64)
+            w_scales[grp] = keep.tile([P, 128 * n], U8, name="ws%d" % grp, align_bytes=64)
+            nc.vector.quantize_mx(out=w_codes[grp][:].bitcast(E4), scales=w_scales[grp][:], in_=w_t[grp][:, 0:n].rearrange("p s v h -> p (s v h)").bitcast(BF16))
+
+        g0s = keep.tile([P, 2, 4, 128], BF16, name="g0s")
+        g_tok = keep.tile([P, 8, 128], BF16, name="g_tok")
+        x_tok = keep.tile([P, 32, 2, 64], BF16, name="x_tok")
+        z_il = keep.tile([P, 2, 128, 4], BF16, name="z_il", align_bytes=64)
+        z_codes = keep.tile([P, 256], U32, name="z_codes", align_bytes=64)
+        z_scales = keep.tile([P, 256], U8, name="z_scales", align_bytes=64)
+
+        def x_tok_fill(copy, g, k0, k1):
+            src = x0[:, g, :, 4 * k0 : 4 * k1].rearrange("p j (k u) -> p k u j", u=4).unsqueeze(2).to_broadcast([P, k1 - k0, 4, 4, 4])
+            copy(out=x_tok[:, k0:k1, g].rearrange("p k (s u j) -> p k s u j", s=4, u=4), in_=src)
+
+        t_vals, t_codes, t_bank = {}, {}, {}
+
+        def codes_tile():
+            c = ring.tile([P, 1024], U32, name="codes", tag="codes", bufs=4, align_bytes=64)
+            s = ring.tile([P, 1024], U8, name="scales", tag="scales", bufs=4, align_bytes=64)
+            return c, s
+
+        def quantize(vals):
+            c, s = codes_tile()
+            nc.vector.quantize_mx(out=c[:].bitcast(E5), scales=s[:], in_=vals)
+            return c, s
+
+        def t_gen(k):
+            t = big([P, 4096], BF16, "tvals")
+            nc.vector.tensor_tensor(
+                out=t[:].rearrange("p (a u c j) -> p a u c j", a=8, u=4, j=4),
+                in0=g_tok[:].rearrange("p a (c j) -> p a c j", j=4).unsqueeze(2).to_broadcast([P, 8, 4, 32, 4]),
+                in1=x_tok[:, k].rearrange("p g (s u j) -> p (g s) u j", s=4, u=4).unsqueeze(3).to_broadcast([P, 8, 4, 32, 4]),
+                op=MULT,
+            )
+            t_vals[k] = t
+
+        def t_q(k):
+            t_codes[k] = quantize(t_vals[k][:])
+
+        def t_mm(k):
+            b = bank("o1bank")
+            c, s = t_codes[k]
+            for g in range(2):
+                nc.tensor.matmul_mx(
+                    out=b[:],
+                    lhsT=z_codes[:, 128 * g : 128 * g + 128].bitcast(E4),
+                    lhsT_scale=z_scales[:, 128 * g : 128 * g + 128],
+                    rhs=c[:, 512 * g : 512 * g + 512].bitcast(E5),
+                    rhs_scale=s[:, 512 * g : 512 * g + 512],
+                    start=(g == 0),
+                    stop=(g == 1),
+                )
+            t_bank[k] = b
+
+        def t_out(k):
+            o = ring.tile([P, 4, 128], F32, name="o1", tag="ostage", bufs=3)
+            nc.scalar.copy(out=o[:].rearrange("p u (c s) -> p (u c) s", s=4), in_=t_bank[k][:].rearrange("p (s q) -> p q s", s=4))
+            nc.sync.dma_start(out=out_1[4 * k : 4 * k + 4].rearrange("u v c -> v u c"), in_=o[:])
+
+        acc = [accp.tile([P, 512], F32, name="acc%d" % g) for g in range(2)]
+        acc_done = [0, 0]
+        acc_total = 32 + 3 + 4 * 8
+        f_vals, f_codes = {}, {}
+
+        def acc_mm(g, cols, grp, s, c, sc, c0):
+            n = cols.stop - cols.start
+            nc.tensor.matmul_mx(
+                out=acc[g][:, cols],
+                lhsT=w_codes[grp][:, 128 * s : 128 * s + 128].bitcast(E4),
+                lhsT_scale=w_scales[grp][:, 128 * s : 128 * s + 128],
+                rhs=c[:, c0 : c0 + n].bitcast(E5),
+                rhs_scale=sc[:, c0 : c0 + n],
+                start=(acc_done[g] == 0),
+                stop=(acc_done[g] == acc_total - 1),
+            )
+            acc_done[g] = acc_done[g] + 1
+
+        def f_q(key):
+            f_codes[key] = quantize(f_vals[key][:])
+
+        def f_mm(key):
+            c, sc = f_codes[key]
+            kind, i = key
+            if kind == "m":
+                for ug in range(8):
+                    acc_mm(i // 4, slice(128 * (i % 4), 128 * (i % 4) + 128), 8 + ug // 4, ug % 4, c, sc, 128 * ug)
+            else:
+                grp, s = (10, i) if kind == "p" else (i // 4, i % 4)
+                for g in range(2):
+                    acc_mm(g, slice(0, 512), grp, s, c, sc, 512 * g)
+
+        r_bank = {}
+
+        def r_tr(k, q):
+            g, h = q // 2, q % 2
+            b = bank("rbank")
+            words = t_vals[k][:].bitcast(F32)
+            for s in range(4):
+                c0 = 1024 * g + 256 * s
+                nc.tensor.transpose(b[:, 128 * s : 128 * s + 128], words[:, c0 + h : c0 + 256 : 2], ident[:])
+            r_bank[k, q] = b
+
+        def r_cp(k, q):
+            if q == 0:
+                f_vals["k", k] = big([P, 4096], BF16, "fvals")
+            nc.scalar.copy(
+                out=f_vals["k", k][:, 1024 * q : 1024 * q + 1024].rearrange("p (e n s) -> p e n s", e=2, s=4),
+                in_=r_bank[k, q][:].bitcast(BF16).rearrange("p (s n e) -> p e n s", s=4, e=2),
+            )
+
+        g_feat = keep.tile([P, 1024, 2], F32, name="g_feat")
+        x_rows = {}
+
+        def d_load(pair):
+            t = ring.tile([P, 2, 1024], F32, name="xrows", tag="xrows")
+            src = park_x.rearrange("(g u k b) c -> g u (k b c)", g=2, u=4, k=16)
+            for u in range(4):
+                nc.sync.dma_start(out=t[32 * u : 32 * u + 32], in_=src[:, u, 1024 * pair : 1024 * pair + 1024].unsqueeze(0).to_broadcast([32, 2, 1024]))
+            x_rows[pair] = t
+
+        def d_gen(kd, g):
+            if g == 0:
+                f_vals["k", 16 + kd] = big([P, 4096], BF16, "fvals")
+            xs2 = x_rows[kd // 2][:, g, 512 * (kd % 2) : 512 * (kd % 2) + 512].bitcast(BF16)
+            nc.vector.tensor_tensor(
+                out=f_vals["k", 16 + kd][:, 2048 * g : 2048 * g + 2048].rearrange("p (n h e) -> p n h e", h=2, e=2),
+                in0=g_feat[:, 512 * g : 512 * g + 512].rearrange("p n h -> p (n h)").bitcast(BF16).rearrange("p (n h e) -> p n h e", h=2, e=2),
+                in1=xs2.rearrange("p (n e) -> p n e", e=2).unsqueeze(2).to_broadcast([P, 512, 2, 2]),
+                op=MULT,
+            )
+
+        mask = keep.tile([P, 16], F32, name="mask")
+        xg = [keep.tile([P, 16, ROW // 2], F32, name="xg%d" % q) for q in range(4)]
+        lhs, m_bank, m_bank2 = {}, {}, {}
+
+        def l_build(c, n0, n1):
+            if n0 == 0:
+                lhs[c] = ring.tile([P, 8, 5, 16, 8], BF16, name="lhs", tag="lhs")
+            src = xg[c // 2][:, 8 * (c % 2) : 8 * (c % 2) + 8].bitcast(BF16)[:, :, 0:40].rearrange("p g (a u) -> p g a u", u=8)
+            for n in range(n0, n1):
+                nc.vector.tensor_scalar(out=lhs[c][:, :, :, n, :], in0=src, scalar1=mask[:, n : n + 1], scalar2=None, op0=MULT)
+
+        def m_mm(grp):
+            b = bank("mbank")
+            rhs = xg[grp // 16][:, grp % 16].bitcast(BF16)
+            for a in range(5):
+                n = 96 if a < 4 else 64
+                nc.tensor.matmul(b[:, 96 * a : 96 * a + n], lhsT=lhs[grp // 8][:, grp % 8, a].rearrange("p n u -> p (n u)"), rhs=rhs[:, 48 : 48 + n], start=True, stop=True)
+            m_bank[grp] = b
+
+        def m_cp(grp):
+            b, d = m_bank[grp], dts[grp % 3]
+            sums = b[:, 0:480].rearrange("p (a w) -> p a w", w=96)
+            nc.scalar.activation(
+                out=d[:, :, 0:160].rearrange("p h (a w) -> p h a w", w=32),
+                in_=sums[:, :, 0:64].rearrange("p a (h w) -> p h a w", h=2),
+                func=COPY,
+                scale=ALPHA1,
+            )
+            nc.scalar.activation(
+                out=d[:, :, 160:224].rearrange("p h (a w) -> p h a w", w=16),
+                in_=sums[:, 0:4, 64:96].rearrange("p a (h w) -> p h a w", h=2),
+                func=COPY,
+                scale=ALPHA2,
+            )
+
+        def m_tr(pair):
+            b = bank("mbank2")
+            for i in range(2):
+                words = dts[(2 * pair + i) % 3][:].bitcast(F32)
+                for h in range(2):
+                    nc.tensor.transpose(b[:, 256 * h + 128 * i : 256 * h + 128 * i + 128], words[:, h], ident[:])
+            m_bank2[pair] = b
+
+        def m_cp2(pair):
+            c = pair // 4
+            if pair % 4 == 0:
+                f_vals["m", c] = ring.tile([P, 4096], BF16, name="fm", tag="fm", align_bytes=64)
+            dst = f_vals["m", c][:].bitcast(F32).rearrange("p (u n h) -> p u n h", u=8, h=2)
+            nc.scalar.copy(out=dst[:, :, 32 * (pair % 4) : 32 * (pair % 4) + 32], in_=m_bank2[pair][:].rearrange("p (h n u) -> p u n h", h=2, u=8))
+
+        g_p = keep.tile([P, 8, 3, 64], BF16, name="g_p")
+        x_p = keep.tile([P, 8, 72], F32, name="x_p")
+        prods, p_bank = {}, {}
+
+        def p_mul(unit):
+            s, t = unit // 8, unit % 8
+            pp = ring.tile([P, 3, 4, 8, 16], F32, name="pp", tag="pp")
+            for m in range(3):
+                for u in range(8):
+                    col = 3 * (8 * s + u) + m
+                    nc.scalar.activation(out=pp[:, m, :, u, :], in_=g_p[:, t, m].rearrange("p (s c) -> p s c", s=4), func=COPY, scale=x_p[:, t, col : col + 1])
+            prods[unit] = pp
+
+        def p_tr(unit):
+            b = bank("pbank")
+            for s in range(4):
+                for m in range(3):
+                    nc.tensor.matmul(b[:, 128 * s : 128 * s + 128], lhsT=prods[unit][:, m, s].rearrange("p u c -> p (u c)"), rhs=ident[:], start=(m == 0), stop=(m == 2), is_transpose=True)
+            p_bank[unit] = b
+
+        def p_cp(unit):
+            s, t = unit // 8, unit % 8
+            if t == 0:
+                f_vals["p", s] = ring.tile([P, 4096], BF16, name="fp", tag="fp", bufs=1, align_bytes=64)
+            nc.scalar.activation(
+                out=f_vals["p", s][:, 512 * t : 512 * t + 512].rearrange("p (n s) -> p n s", s=4),
+                in_=p_bank[unit][:].rearrange("p (s n) -> p n s", s=4),
+                func=COPY,
+                scale=ALPHA1,
+            )
+
+        w_load(0)
+        nc.vector.tensor_scalar(out=g0s[:].rearrange("p g j c -> p (g j c)"), in0=g0[:].rearrange("p g j c -> p (g j c)"), scalar1=ALPHA0, scalar2=None, op0=MULT)
+        x_tok_fill(nc.vector.tensor_copy, 0, 0, 4)
+        x_tok_fill(nc.scalar.copy, 1, 0, 4)
+        nc.vector.tensor_copy(out=g_tok[:].rearrange("p (g s) (c j) -> p g s c j", g=2, j=4), in_=g0s[:].rearrange("p g j (c s) -> p g s c j", s=4))
+        nc.vector.tensor_copy(out=z_il[:], in_=zin[:].rearrange("p g j v -> p g v j"))
+        x_dup = big([P, 4, 2, 64, 2], BF16, "x_dup")
+        for g in range(2):
+            src = x0[:, g, :, 64:128].rearrange("p j (k u) -> p j u k", u=4).unsqueeze(4).to_broadcast([P, 4, 4, 16, 2])
+            nc.scalar.copy(out=x_dup[:, :, g].rearrange("p j (u k) e -> p j u k e", u=4), in_=src)
+        xb = bank("xbank")
+        for j in range(4):
+            nc.tensor.transpose(xb[:, 128 * j : 128 * j + 128], x_dup[:, j].rearrange("p g q e -> p (g q e)").bitcast(F32), ident[:])
+        for g in range(2):
+            t = pm[g]
+            nc.scalar.copy(out=t[:, :, 0:3, 0:40], in_=xr[:, g, :, 0:120].rearrange("p j (u r) -> p j r u", r=3))
+            nc.scalar.copy(out=t[:, :, 3:8, 0:32], in_=xr[:, g, :, 192:352].rearrange("p j (u r) -> p j r u", r=5))
+            for h in range(2):
+                nc.scalar.copy(
+                    out=t[:, :, 0:3, 48 + 32 * h : 80 + 32 * h].rearrange("p j r (c e) -> p j r c e", e=2),
+                    in_=gr[:, g, :, 0:192].rearrange("p j (c h e r) -> p h j r c e", h=2, e=2, r=3)[:, h],
+                )
+                nc.scalar.copy(
+                    out=t[:, :, 3:8, 112 + 16 * h : 128 + 16 * h].rearrange("p j r (c e) -> p j r c e", e=2),
+                    in_=gr[:, g, :, 192:352].rearrange("p j (c h e r) -> p h j r c e", h=2, e=2, r=5)[:, h],
+                )
+            nc.sync.dma_start(out=park_m.rearrange("(g j p w) -> g p j w", g=2, j=4, p=P)[g], in_=t[:].rearrange("p j r w -> p j (r w)").bitcast(F32))
+            if g == 0:
+                x_t = ring.tile([P, 512], F32, name="x_t", tag="ostage", bufs=3)
+                nc.scalar.copy(out=x_t[:], in_=xb[:])
+                nc.sync.dma_start(out=park_x.rearrange("(a b) c -> a (b c)", a=P), in_=x_t[:])
+        w_load(4)
+        for q in range(4):
+            nc.sync.dma_start(out=xg[q][:], in_=park_m.rearrange("(g k w) -> k g w", k=P, w=ROW // 2)[:, 16 * q : 16 * q + 16])
+        d_load(0)
+        nc.vector.tensor_reduce(out=mask[:], in_=ident[:].rearrange("p (n r) -> p n r", r=8), axis=mybir.AxisListType.X, op=ADD)
+        nc.vector.quantize_mx(out=z_codes[:].bitcast(E4), scales=z_scales[:], in_=z_il[:].rearrange("p g v j -> p (g v j)"))
+
+        def g_feat_fill():
+            g_rep = big([P, 8, 2, 128], F32, "g_rep")
+            src = g0s[:].rearrange("p g j c -> p (g j) c").bitcast(F32).rearrange("p t (c h) -> p t h c", h=2).unsqueeze(3).to_broadcast([P, 8, 2, 4, 32])
+            nc.scalar.copy(out=g_rep[:].rearrange("p t h (u c) -> p t h u c", u=4), in_=src)
+            for q in range(4):
+                b = bank("gbank")
+                for i in range(4):
+                    nc.tensor.transpose(b[:, 128 * i : 128 * i + 128], g_rep[:, 2 * q + i // 2, i % 2], ident[:])
+                nc.scalar.copy(out=g_feat[:, 256 * q : 256 * q + 256].rearrange("p (t n) h -> p t n h", t=2), in_=b[:].rearrange("p (t h n) -> p t n h", t=2, h=2))
+
+        def p_fill():
+            nc.scalar.copy(out=g_p[:].rearrange("p t m (s c) -> p t m s c", s=4), in_=gr[:, :, :, 0:192].rearrange("p g j (c s m) -> p (g j) m s c", s=4, m=3))
+            nc.scalar.copy(out=x_p[:], in_=xr[:, :, :, 120:192].rearrange("p g j w -> p (g j) w"))
+
+        r_steps = [0, 1, 2] + list(range(4, 29, 2))
+        other_steps = [s for s in range(STEPS) if s not in r_steps]
+        k_of = {s: i for i, s in enumerate(r_steps)}
+        k_of.update({s: 16 + i for i, s in enumerate(other_steps)})
+        d_at = {s: [] for s in range(STEPS)}
+        for kd, s in enumerate(list(range(3, 28, 2)) + [28, 29, 30]):
+            d_at[s].append(kd)
+        m_at = {s: [q for q in range(32) if 3 + q * 26 // 32 == s] for s in range(STEPS)}
+        l_at = {s: [c for c in range(8) if 3 + 4 * c * 26 // 32 == s + 1] for s in range(STEPS)}
+        p_at = {s: ([s - 3, s - 2] if s % 2 == 1 and 3 <= s <= 25 else []) for s in range(STEPS)}
+        w_at = {1: 4, 2: 8, 3: 9, 4: 1, 6: 10, 8: 5, 12: 2, 16: 6, 20: 3, 24: 7}
+        w_load_at = {0: 8, 2: 9, 3: 1, 4: 10, 6: 5, 10: 2, 14: 6, 18: 3, 22: 7}
+
+        for half in range(2):
+            w_tr(0, half)
+            w_cp(0, half)
+        early, late, ready = [], [], []
+        for s in range(STEPS):
+            k = k_of[s]
+            routed = s in r_steps
+            t_gen(k)
+            if s in w_load_at:
+                w_load(w_load_at[s])
+            for key in ready:
+                f_mm(key)
+            ready = []
+            if routed:
+                r_tr(k, 0)
+                r_tr(k, 1)
+            if s == 0:
+                w_q(0)
+            for key in early:
+                f_q(key)
+            if routed:
+                r_cp(k, 0)
+                r_cp(k, 1)
+            for u in p_at[s][:1]:
+                p_mul(u)
+            for q in m_at[s][:1]:
+                m_mm(2 * q)
+                m_mm(2 * q + 1)
+            t_q(k)
+            for key in early:
+                f_mm(key)
+            early = []
+            if routed:
+                r_tr(k, 2)
+                r_tr(k, 3)
+            for u in p_at[s][:1]:
+                p_tr(u)
+            for q in m_at[s][:1]:
+                m_cp(2 * q)
+                m_cp(2 * q + 1)
+            if routed:
+                r_cp(k, 2)
+                r_cp(k, 3)
+            for u in p_at[s][1:]:
+                p_mul(u)
+            for kd in d_at[s]:
+                d_gen(kd, 0)
+            for c in l_at[s]:
+                l_build(c, 0, 16)
+            for kd in d_at[s]:
+                d_gen(kd, 1)
+                early.append(("k", 16 + kd))
+                if kd % 2 == 0 and kd < 14:
+                    d_load(kd // 2 + 1)
+            t_mm(k)
+            for q in m_at[s][:1]:
+                m_tr(q)
+            for u in p_at[s][:1]:
+                p_cp(u)
+            for u in p_at[s][1:]:
+                p_tr(u)
+            t_out(k)
+            for q in m_at[s][:1]:
+                m_cp2(q)
+            for u in p_at[s][1:]:
+                p_cp(u)
+                if u % 8 == 7:
+                    early.append(("p", u // 8))
+            for q in m_at[s][1:]:
+                m_mm(2 * q)
+                m_mm(2 * q + 1)
+                m_cp(2 * q)
+                m_cp(2 * q + 1)
+                m_tr(q)
+                m_cp2(q)
+            for q in m_at[s]:
+                if q % 4 == 3:
+                    early.append(("m", q // 4))
+            if s in w_at:
+                for half in range(2):
+                    w_tr(w_at[s], half)
+                    w_cp(w_at[s], half)
+            for key in late:
+                f_q(key)
+                ready.append(key)
+            late = [("k", k)] if routed else []
+            if s in w_at:
+                w_q(w_at[s])
+            if s == 0:
+                for g in range(2):
+                    x_tok_fill(nc.scalar.copy, g, 16, 20)
+                g_feat_fill()
+            if s == 1:
+                p_fill()
+            if s == 2:
+                for g in range(2):
+                    x_tok_fill(nc.scalar.copy, g, 4, 16)
+            if s == 4:
+                for g in range(2):
+                    x_tok_fill(nc.scalar.copy, g, 20, 32)
+        for key in early:
+            f_q(key)
+            f_mm(key)
+
+        for g in range(2):
+            a_sb = ring.tile([P, 512], F32, name="a_sb", tag="ostage", bufs=3)
+            if g == 0:
+                nc.scalar.copy(out=a_sb[:], in_=acc[g][:])
+            else:
+                nc.vector.tensor_copy(out=a_sb[:], in_=acc[g][:])
+            b = bank("obank")
+            for j in range(4):
+                nc.tensor.transpose(b[:, 128 * j : 128 * j + 128], a_sb[:, 128 * j : 128 * j + 128], ident[:])
+            o = ring.tile([P, 512], F32, name="o0", tag="pp")
+            if g == 0:
+                nc.scalar.copy(out=o[:], in_=b[:])
+            else:
+                nc.vector.tensor_copy(out=o[:], in_=b[:])
+            nc.sync.dma_start(out=out_0.rearrange("(g p j) v -> g p (j v)", g=2, j=4)[g], in_=o[:])

@@ -21,7 +21,8 @@ ALPHA0 = 1.0 / 128
 ALPHA1 = 1.0 / math.sqrt(64 * 128)
 ALPHA2 = 1.0 / 64
 ROW = 144
-STEPS = 32
+DIRECT = 20
+ROUTED = 32 - DIRECT
 
 
 def tile_selfconnectionintro_v_kernel(tc, x, z, w0, w1, w2, grad_out, out_0, out_1):
@@ -31,9 +32,10 @@ def tile_selfconnectionintro_v_kernel(tc, x, z, w0, w1, w2, grad_out, out_0, out
         ring = ctx.enter_context(tc.tile_pool(name="ring", bufs=2))
         accp = ctx.enter_context(tc.psum_pool(name="accp", bufs=1))
         psum = ctx.enter_context(tc.psum_pool(name="psum", bufs=6))
+        ctx.enter_context(tc.manual_schedule())
 
         def big(shape, dtype, name):
-            t = ring.tile(shape, dtype, name=name, tag="big", bufs=4, align_bytes=64)
+            t = ring.tile(shape, dtype, name=name, tag="big", bufs=5, align_bytes=64)
             return t
 
         def bank(name):
@@ -42,21 +44,20 @@ def tile_selfconnectionintro_v_kernel(tc, x, z, w0, w1, w2, grad_out, out_0, out
 
         x_v = x.rearrange("(g p j) w -> g p j w", g=2, j=4)
         g_v = grad_out.rearrange("(g p j) w -> g p j w", g=2, j=4)
-        park_x = out_0[0:512, :]
+        park_x = out_0[0 : 32 * DIRECT, :]
         park_m = out_1[92:128].rearrange("u v c -> (u v c)")
 
-        g0 = keep.tile([P, 2, 4, 128], BF16, name="g0")
-        x0 = keep.tile([P, 2, 4, 128], BF16, name="x0")
+        first = ring.tile([P, 3, 2, 4, 128], BF16, name="first", tag="pp")
+        g0, x0, zin = first[:, 0], first[:, 1], first[:, 2]
         for g in range(2):
             nc.sync.dma_start(out=g0[:, g], in_=g_v[g, :, :, 0:128])
             nc.sync.dma_start(out=x0[:, g], in_=x_v[g, :, :, 0:128])
-        zin = keep.tile([P, 2, 4, 128], BF16, name="zin")
-        nc.sync.dma_start(out=zin[:].rearrange("p g j v -> p g (j v)"), in_=z.rearrange("(g p j) v -> p g (j v)", g=2, j=4))
         xr = ring.tile([P, 2, 4, 352], BF16, name="xr", tag="fm", align_bytes=64)
         gr = ring.tile([P, 2, 4, 352], BF16, name="gr", tag="fm", align_bytes=64)
         for g in range(2):
             nc.sync.dma_start(out=xr[:, g], in_=x_v[g, :, :, 128:480])
             nc.sync.dma_start(out=gr[:, g], in_=g_v[g, :, :, 128:480])
+        nc.sync.dma_start(out=zin.rearrange("p g j v -> p g (j v)"), in_=z.rearrange("(g p j) v -> p g (j v)", g=2, j=4))
 
         ident = keep.tile([P, P], F32, name="ident")
         make_identity(nc, ident[:])
@@ -66,7 +67,7 @@ def tile_selfconnectionintro_v_kernel(tc, x, z, w0, w1, w2, grad_out, out_0, out
             nc.gpsimd.memset(t[:].rearrange("p j r w -> p (j r w)").bitcast(F32), 0.0)
             pm.append(t)
         dts = []
-        for i in range(3):
+        for i in range(4):
             t = keep.tile([P, 2, 256], BF16, name="dstage%d" % i)
             nc.gpsimd.memset(t[:, :, 224:256], 0.0)
             dts.append(t)
@@ -81,16 +82,16 @@ def tile_selfconnectionintro_v_kernel(tc, x, z, w0, w1, w2, grad_out, out_0, out
                 t = ring.tile([P, 16, 128], BF16, name="wraw", tag="wraw")
                 nc.sync.dma_start(out=t[:], in_=w0[16 * grp : 16 * grp + 16].rearrange("u v c -> v u c"))
                 w_raw[grp] = t[:].rearrange("p u c -> p (u c)").bitcast(F32)
-            elif grp < 10:
-                t = ring.tile([P, 4, 512], BF16, name="wraw", tag="wraw")
-                nc.gpsimd.memset(t[:, :, 448:512], 0.0)
-                ug0 = 4 * (grp - 8)
+            elif grp == 8:
+                t = big([P, 8, 512], BF16, "w_mix")
+                nc.vector.memset(t[:, :, 448:512], 0.0)
                 for a in range(5):
-                    nc.sync.dma_start(out=t[:, :, 64 * a : 64 * a + 64], in_=w1[8 * a + ug0 : 8 * a + ug0 + 4].rearrange("u v c -> v u c"))
+                    nc.sync.dma_start(out=t[:, :, 64 * a : 64 * a + 64], in_=w1[8 * a : 8 * a + 8].rearrange("u v c -> v u c"))
                 for a in range(4):
-                    nc.sync.dma_start(out=t[:, :, 320 + 32 * a : 352 + 32 * a], in_=w2[8 * a + ug0 : 8 * a + ug0 + 4].rearrange("u v c -> v u c"))
-                w_raw[grp] = t[:].rearrange("p u c -> p (u c)").bitcast(F32)
-            else:
+                    nc.sync.dma_start(out=t[:, :, 320 + 32 * a : 352 + 32 * a], in_=w2[8 * a : 8 * a + 8].rearrange("u v c -> v u c"))
+                for i in range(2):
+                    w_raw[8 + i] = t[:, 4 * i : 4 * i + 4].rearrange("p u c -> p (u c)").bitcast(F32)
+            elif grp == 10:
                 t = ring.tile([P, 24, 64], BF16, name="wraw", tag="wraw")
                 nc.sync.dma_start(out=t[:], in_=w1[40:64].rearrange("u v c -> v u c"))
                 w_raw[grp] = t[:].rearrange("p u c -> p (u c)").bitcast(F32)
@@ -122,9 +123,7 @@ def tile_selfconnectionintro_v_kernel(tc, x, z, w0, w1, w2, grad_out, out_0, out
         z_codes = keep.tile([P, 256], U32, name="z_codes", align_bytes=64)
         z_scales = keep.tile([P, 256], U8, name="z_scales", align_bytes=64)
 
-        def x_tok_fill(copy, g, k0, k1):
-            src = x0[:, g, :, 4 * k0 : 4 * k1].rearrange("p j (k u) -> p k u j", u=4).unsqueeze(2).to_broadcast([P, k1 - k0, 4, 4, 4])
-            copy(out=x_tok[:, k0:k1, g].rearrange("p k (s u j) -> p k s u j", s=4, u=4), in_=src)
+        x_il = keep.tile([P, 2, 128, 4], BF16, name="x_il")
 
         t_vals, t_codes, t_bank = {}, {}, {}
 
@@ -225,23 +224,22 @@ def tile_selfconnectionintro_v_kernel(tc, x, z, w0, w1, w2, grad_out, out_0, out
         g_feat = keep.tile([P, 1024, 2], F32, name="g_feat")
         x_rows = {}
 
-        def d_load(pair):
-            t = ring.tile([P, 2, 1024], F32, name="xrows", tag="xrows")
-            src = park_x.rearrange("(g u k b) c -> g u (k b c)", g=2, u=4, k=16)
+        def d_load(kd):
+            t = ring.tile([P, 8, 128], F32, name="xrows", tag="xrows", bufs=3)
+            src = park_x.rearrange("(t u k) n -> u k t n", t=8, u=4)
             for u in range(4):
-                nc.sync.dma_start(out=t[32 * u : 32 * u + 32], in_=src[:, u, 1024 * pair : 1024 * pair + 1024].unsqueeze(0).to_broadcast([32, 2, 1024]))
-            x_rows[pair] = t
+                nc.sync.dma_start(out=t[32 * u : 32 * u + 32], in_=src[u, kd].unsqueeze(0).to_broadcast([32, 8, 128]))
+            x_rows[kd] = t
 
-        def d_gen(kd, g):
-            if g == 0:
-                f_vals["k", 16 + kd] = big([P, 4096], BF16, "fvals")
-            xs2 = x_rows[kd // 2][:, g, 512 * (kd % 2) : 512 * (kd % 2) + 512].bitcast(BF16)
+        def d_gen(kd):
+            t = big([P, 4096], BF16, "fvals")
             nc.vector.tensor_tensor(
-                out=f_vals["k", 16 + kd][:, 2048 * g : 2048 * g + 2048].rearrange("p (n h e) -> p n h e", h=2, e=2),
-                in0=g_feat[:, 512 * g : 512 * g + 512].rearrange("p n h -> p (n h)").bitcast(BF16).rearrange("p (n h e) -> p n h e", h=2, e=2),
-                in1=xs2.rearrange("p (n e) -> p n e", e=2).unsqueeze(2).to_broadcast([P, 512, 2, 2]),
+                out=t[:].rearrange("p (n h e) -> p n h e", h=2, e=2),
+                in0=g_feat[:].rearrange("p n h -> p (n h)").bitcast(BF16).rearrange("p (n h e) -> p n h e", h=2, e=2),
+                in1=x_rows[kd][:].rearrange("p t n -> p (t n)").bitcast(BF16).rearrange("p (n e) -> p n e", e=2).unsqueeze(2).to_broadcast([P, 1024, 2, 2]),
                 op=MULT,
             )
+            f_vals["k", ROUTED + kd] = t
 
         mask = keep.tile([P, 16], F32, name="mask")
         xg = [keep.tile([P, 16, ROW // 2], F32, name="xg%d" % q) for q in range(4)]
@@ -263,7 +261,7 @@ def tile_selfconnectionintro_v_kernel(tc, x, z, w0, w1, w2, grad_out, out_0, out
             m_bank[grp] = b
 
         def m_cp(grp):
-            b, d = m_bank[grp], dts[grp % 3]
+            b, d = m_bank[grp], dts[grp % 4]
             sums = b[:, 0:480].rearrange("p (a w) -> p a w", w=96)
             nc.scalar.activation(
                 out=d[:, :, 0:160].rearrange("p h (a w) -> p h a w", w=32),
@@ -281,7 +279,7 @@ def tile_selfconnectionintro_v_kernel(tc, x, z, w0, w1, w2, grad_out, out_0, out
         def m_tr(pair):
             b = bank("mbank2")
             for i in range(2):
-                words = dts[(2 * pair + i) % 3][:].bitcast(F32)
+                words = dts[(2 * pair + i) % 4][:].bitcast(F32)
                 for h in range(2):
                     nc.tensor.transpose(b[:, 256 * h + 128 * i : 256 * h + 128 * i + 128], words[:, h], ident[:])
             m_bank2[pair] = b
@@ -316,7 +314,7 @@ def tile_selfconnectionintro_v_kernel(tc, x, z, w0, w1, w2, grad_out, out_0, out
         def p_cp(unit):
             s, t = unit // 8, unit % 8
             if t == 0:
-                f_vals["p", s] = ring.tile([P, 4096], BF16, name="fp", tag="fp", bufs=1, align_bytes=64)
+                f_vals["p", s] = ring.tile([P, 4096], BF16, name="fp", tag="fp", align_bytes=64)
             nc.scalar.activation(
                 out=f_vals["p", s][:, 512 * t : 512 * t + 512].rearrange("p (n s) -> p n s", s=4),
                 in_=p_bank[unit][:].rearrange("p (s n) -> p n s", s=4),
@@ -324,20 +322,22 @@ def tile_selfconnectionintro_v_kernel(tc, x, z, w0, w1, w2, grad_out, out_0, out
                 scale=ALPHA1,
             )
 
-        w_load(0)
-        nc.vector.tensor_scalar(out=g0s[:].rearrange("p g j c -> p (g j c)"), in0=g0[:].rearrange("p g j c -> p (g j c)"), scalar1=ALPHA0, scalar2=None, op0=MULT)
-        x_tok_fill(nc.vector.tensor_copy, 0, 0, 4)
-        x_tok_fill(nc.scalar.copy, 1, 0, 4)
-        nc.vector.tensor_copy(out=g_tok[:].rearrange("p (g s) (c j) -> p g s c j", g=2, j=4), in_=g0s[:].rearrange("p g j (c s) -> p g s c j", s=4))
-        nc.vector.tensor_copy(out=z_il[:], in_=zin[:].rearrange("p g j v -> p g v j"))
-        x_dup = big([P, 4, 2, 64, 2], BF16, "x_dup")
-        for g in range(2):
-            src = x0[:, g, :, 64:128].rearrange("p j (k u) -> p j u k", u=4).unsqueeze(4).to_broadcast([P, 4, 4, 16, 2])
-            nc.scalar.copy(out=x_dup[:, :, g].rearrange("p j (u k) e -> p j u k e", u=4), in_=src)
-        xb = bank("xbank")
-        for j in range(4):
-            nc.tensor.transpose(xb[:, 128 * j : 128 * j + 128], x_dup[:, j].rearrange("p g q e -> p (g q e)").bitcast(F32), ident[:])
-        for g in range(2):
+        def x_park():
+            x_dup = big([P, 8, 4, DIRECT, 2], BF16, "x_dup")
+            src = x0[:, :, :, 4 * ROUTED : 128].rearrange("p g j (k u) -> p (g j) u k", u=4).unsqueeze(4).to_broadcast([P, 8, 4, DIRECT, 2])
+            nc.scalar.copy(out=x_dup[:], in_=src)
+            words = x_dup[:].rearrange("p t u k e -> p (t u k e)").bitcast(F32)
+            blocks = DIRECT // 4
+            for i0 in range(0, blocks, 4):
+                n = min(4, blocks - i0)
+                b = bank("xbank")
+                for i in range(n):
+                    nc.tensor.transpose(b[:, 128 * i : 128 * i + 128], words[:, 128 * (i0 + i) : 128 * (i0 + i) + 128], ident[:])
+                x_t = ring.tile([P, 512], F32, name="x_t", tag="ostage", bufs=3)
+                nc.scalar.copy(out=x_t[:, 0 : 128 * n], in_=b[:, 0 : 128 * n])
+                nc.sync.dma_start(out=park_x[128 * i0 : 128 * (i0 + n)].rearrange("(i p) n -> p i n", p=P), in_=x_t[:, 0 : 128 * n].rearrange("p (i n) -> p i n", n=128))
+
+        def m_park(g):
             t = pm[g]
             nc.scalar.copy(out=t[:, :, 0:3, 0:40], in_=xr[:, g, :, 0:120].rearrange("p j (u r) -> p j r u", r=3))
             nc.scalar.copy(out=t[:, :, 3:8, 0:32], in_=xr[:, g, :, 192:352].rearrange("p j (u r) -> p j r u", r=5))
@@ -351,16 +351,22 @@ def tile_selfconnectionintro_v_kernel(tc, x, z, w0, w1, w2, grad_out, out_0, out
                     in_=gr[:, g, :, 192:352].rearrange("p j (c h e r) -> p h j r c e", h=2, e=2, r=5)[:, h],
                 )
             nc.sync.dma_start(out=park_m.rearrange("(g j p w) -> g p j w", g=2, j=4, p=P)[g], in_=t[:].rearrange("p j r w -> p j (r w)").bitcast(F32))
-            if g == 0:
-                x_t = ring.tile([P, 512], F32, name="x_t", tag="ostage", bufs=3)
-                nc.scalar.copy(out=x_t[:], in_=xb[:])
-                nc.sync.dma_start(out=park_x.rearrange("(a b) c -> a (b c)", a=P), in_=x_t[:])
-        w_load(4)
-        for q in range(4):
+
+        def xg_load(q):
             nc.sync.dma_start(out=xg[q][:], in_=park_m.rearrange("(g k w) -> k g w", k=P, w=ROW // 2)[:, 16 * q : 16 * q + 16])
-        d_load(0)
-        nc.vector.tensor_reduce(out=mask[:], in_=ident[:].rearrange("p (n r) -> p n r", r=8), axis=mybir.AxisListType.X, op=ADD)
-        nc.vector.quantize_mx(out=z_codes[:].bitcast(E4), scales=z_scales[:], in_=z_il[:].rearrange("p g v j -> p (g v j)"))
+
+        def t_fill():
+            nc.vector.tensor_scalar(out=g0s[:].rearrange("p g j c -> p (g j c)"), in0=g0.rearrange("p g j c -> p (g j c)"), scalar1=ALPHA0, scalar2=None, op0=MULT)
+            nc.vector.tensor_copy(out=x_il[:], in_=x0.rearrange("p g j u -> p g u j"))
+            nc.vector.tensor_copy(out=g_tok[:].rearrange("p (g s) (c j) -> p g s c j", g=2, j=4), in_=g0s[:].rearrange("p g j (c s) -> p g s c j", s=4))
+            for g in range(2):
+                src = x_il[:, g].rearrange("p (k u) j -> p k (u j)", u=4).unsqueeze(2).to_broadcast([P, 32, 4, 16])
+                nc.vector.tensor_copy(out=x_tok[:, :, g].rearrange("p k (s q) -> p k s q", s=4), in_=src)
+
+        def z_fill():
+            nc.vector.tensor_copy(out=z_il[:], in_=zin.rearrange("p g j v -> p g v j"))
+            nc.vector.tensor_reduce(out=mask[:], in_=ident[:].rearrange("p (n r) -> p n r", r=8), axis=mybir.AxisListType.X, op=ADD)
+            nc.vector.quantize_mx(out=z_codes[:].bitcast(E4), scales=z_scales[:], in_=z_il[:].rearrange("p g v j -> p (g v j)"))
 
         def g_feat_fill():
             g_rep = big([P, 8, 2, 128], F32, "g_rep")
@@ -376,135 +382,153 @@ def tile_selfconnectionintro_v_kernel(tc, x, z, w0, w1, w2, grad_out, out_0, out
             nc.scalar.copy(out=g_p[:].rearrange("p t m (s c) -> p t m s c", s=4), in_=gr[:, :, :, 0:192].rearrange("p g j (c s m) -> p (g j) m s c", s=4, m=3))
             nc.scalar.copy(out=x_p[:], in_=xr[:, :, :, 120:192].rearrange("p g j w -> p (g j) w"))
 
-        r_steps = [0, 1, 2] + list(range(4, 29, 2))
-        other_steps = [s for s in range(STEPS) if s not in r_steps]
-        k_of = {s: i for i, s in enumerate(r_steps)}
-        k_of.update({s: 16 + i for i, s in enumerate(other_steps)})
-        d_at = {s: [] for s in range(STEPS)}
-        for kd, s in enumerate(list(range(3, 28, 2)) + [28, 29, 30]):
-            d_at[s].append(kd)
-        m_at = {s: [q for q in range(32) if 3 + q * 26 // 32 == s] for s in range(STEPS)}
-        l_at = {s: [c for c in range(8) if 3 + 4 * c * 26 // 32 == s + 1] for s in range(STEPS)}
-        p_at = {s: ([s - 3, s - 2] if s % 2 == 1 and 3 <= s <= 25 else []) for s in range(STEPS)}
-        w_at = {1: 4, 2: 8, 3: 9, 4: 1, 6: 10, 8: 5, 12: 2, 16: 6, 20: 3, 24: 7}
-        w_load_at = {0: 8, 2: 9, 3: 1, 4: 10, 6: 5, 10: 2, 14: 6, 18: 3, 22: 7}
-
-        for half in range(2):
-            w_tr(0, half)
-            w_cp(0, half)
-        early, late, ready = [], [], []
-        for s in range(STEPS):
-            k = k_of[s]
-            routed = s in r_steps
-            t_gen(k)
-            if s in w_load_at:
-                w_load(w_load_at[s])
-            for key in ready:
-                f_mm(key)
-            ready = []
-            if routed:
-                r_tr(k, 0)
-                r_tr(k, 1)
-            if s == 0:
-                w_q(0)
-            for key in early:
-                f_q(key)
-            if routed:
-                r_cp(k, 0)
-                r_cp(k, 1)
-            for u in p_at[s][:1]:
-                p_mul(u)
-            for q in m_at[s][:1]:
-                m_mm(2 * q)
-                m_mm(2 * q + 1)
-            t_q(k)
-            for key in early:
-                f_mm(key)
-            early = []
-            if routed:
-                r_tr(k, 2)
-                r_tr(k, 3)
-            for u in p_at[s][:1]:
-                p_tr(u)
-            for q in m_at[s][:1]:
-                m_cp(2 * q)
-                m_cp(2 * q + 1)
-            if routed:
-                r_cp(k, 2)
-                r_cp(k, 3)
-            for u in p_at[s][1:]:
-                p_mul(u)
-            for kd in d_at[s]:
-                d_gen(kd, 0)
-            for c in l_at[s]:
-                l_build(c, 0, 16)
-            for kd in d_at[s]:
-                d_gen(kd, 1)
-                early.append(("k", 16 + kd))
-                if kd % 2 == 0 and kd < 14:
-                    d_load(kd // 2 + 1)
-            t_mm(k)
-            for q in m_at[s][:1]:
-                m_tr(q)
-            for u in p_at[s][:1]:
-                p_cp(u)
-            for u in p_at[s][1:]:
-                p_tr(u)
-            t_out(k)
-            for q in m_at[s][:1]:
-                m_cp2(q)
-            for u in p_at[s][1:]:
-                p_cp(u)
-                if u % 8 == 7:
-                    early.append(("p", u // 8))
-            for q in m_at[s][1:]:
-                m_mm(2 * q)
-                m_mm(2 * q + 1)
-                m_cp(2 * q)
-                m_cp(2 * q + 1)
-                m_tr(q)
-                m_cp2(q)
-            for q in m_at[s]:
-                if q % 4 == 3:
-                    early.append(("m", q // 4))
-            if s in w_at:
-                for half in range(2):
-                    w_tr(w_at[s], half)
-                    w_cp(w_at[s], half)
-            for key in late:
-                f_q(key)
-                ready.append(key)
-            late = [("k", k)] if routed else []
-            if s in w_at:
-                w_q(w_at[s])
-            if s == 0:
-                for g in range(2):
-                    x_tok_fill(nc.scalar.copy, g, 16, 20)
-                g_feat_fill()
-            if s == 1:
-                p_fill()
-            if s == 2:
-                for g in range(2):
-                    x_tok_fill(nc.scalar.copy, g, 4, 16)
-            if s == 4:
-                for g in range(2):
-                    x_tok_fill(nc.scalar.copy, g, 20, 32)
-        for key in early:
-            f_q(key)
-            f_mm(key)
-
-        for g in range(2):
-            a_sb = ring.tile([P, 512], F32, name="a_sb", tag="ostage", bufs=3)
-            if g == 0:
-                nc.scalar.copy(out=a_sb[:], in_=acc[g][:])
-            else:
-                nc.vector.tensor_copy(out=a_sb[:], in_=acc[g][:])
+        def out0_turn(g):
+            a_sb = ring.tile([P, 512], F32, name="a_sb", tag="pp")
+            nc.scalar.copy(out=a_sb[:], in_=acc[g][:])
             b = bank("obank")
             for j in range(4):
                 nc.tensor.transpose(b[:, 128 * j : 128 * j + 128], a_sb[:, 128 * j : 128 * j + 128], ident[:])
-            o = ring.tile([P, 512], F32, name="o0", tag="pp")
-            if g == 0:
-                nc.scalar.copy(out=o[:], in_=b[:])
-            else:
-                nc.vector.tensor_copy(out=o[:], in_=b[:])
+            return b
+
+        def out0_store(g, b):
+            o = ring.tile([P, 512], F32, name="o0", tag="xrows", bufs=3)
+            nc.scalar.copy(out=o[:], in_=b[:])
             nc.sync.dma_start(out=out_0.rearrange("(g p j) v -> g p (j v)", g=2, j=4)[g], in_=o[:])
+
+        first_t, last_t = 3, 2
+        mid = 32 - first_t - last_t
+        units = [("t", None)] * first_t
+        for i in range(DIRECT):
+            units.append(("d", i))
+            units.extend([("t", None)] * ((i + 1) * mid // DIRECT - i * mid // DIRECT))
+        units.extend([("t", None)] * last_t)
+        t_slots = [i for i, u in enumerate(units) if u[0] == "t"]
+        inner = t_slots[first_t : 32 - last_t - 2]
+        routed_slots = [inner[(2 * r + 1) * len(inner) // (2 * ROUTED)] for r in range(ROUTED)]
+        plain_k = list(range(ROUTED, 32))
+        for i in t_slots:
+            units[i] = ("t", routed_slots.index(i) if i in routed_slots else plain_k.pop(0))
+        slots = len(units)
+        m0, m1 = 8, slots - 4
+        m_at = {m0 + q * (m1 - m0) // 32: q for q in range(32)}
+        free = [i for i in range(2, slots - 4) if i - 1 not in routed_slots]
+        p_at = {free[u * len(free) // 24]: u for u in range(24)}
+        need = {}
+        for i, (kind, k) in enumerate(units):
+            if kind == "d":
+                need.setdefault((ROUTED + k) // 4, i + 1)
+            elif k < ROUTED:
+                need.setdefault(k // 4, i + 4)
+        need[8], need[9], need[10] = m0 + 6, m0 + 7, m0 + 8
+        w_at = {}
+        for grp in sorted(need, key=lambda q: -need[q]):
+            i = need[grp] - 4
+            while i in w_at or i + 1 in w_at:
+                i = i - 1
+            w_at[i] = grp
+        w_order = [w_at[i] for i in sorted(w_at)]
+        loads = [grp for grp in w_order if grp != 9]
+        w_load(loads[0])
+        t_fill()
+        x_park()
+        d_load(0)
+        g_feat_fill()
+        p_fill()
+        d_load(1)
+        loads = [grp for grp in loads[1:] if grp != 8]
+        w_load(loads.pop(0))
+
+        made, quantized, later, turned = [], [], {}, []
+        for i in range(slots + 2):
+            kind, k = units[i] if i < slots else (None, None)
+            if kind == "t":
+                t_gen(k)
+            if kind == "d":
+                d_gen(k)
+                if k + 2 < DIRECT:
+                    d_load(k + 2)
+            if i == 1:
+                z_fill()
+                m_park(0)
+                xg_load(0)
+            if i == 3:
+                m_park(1)
+            if i == m0 - 4:
+                w_load(8)
+            if m_at.get(i) in (0, 6, 14):
+                xg_load((m_at[i] + 10) // 8)
+            done = quantized
+            quantized = []
+            for key in done:
+                if key[0] == "t":
+                    t_mm(key[1])
+                else:
+                    f_mm(key)
+            q = m_at.get(i)
+            if q is not None:
+                m_mm(2 * q)
+                m_mm(2 * q + 1)
+            for key in made + later.get(i, []):
+                if key[0] == "t":
+                    t_q(key[1])
+                    quantized.append(key)
+                elif key[0] == "w":
+                    w_q(key[1])
+                else:
+                    f_q(key)
+                    quantized.append(key)
+            made = [("t", k) if kind == "t" else ("k", ROUTED + k)] if i < slots else []
+            for lead in (1, 2):
+                c = m_at.get(i + lead)
+                if c is not None and c % 4 == 0:
+                    l_build(c // 4, 16 - 8 * lead, 24 - 8 * lead)
+            r = units[i - 1][1] if i - 1 in routed_slots else None
+            u_prev = p_at.get(i - 1)
+            for key in done:
+                if key[0] == "t":
+                    t_out(key[1])
+            q_prev = m_at.get(i - 1)
+            if q_prev is not None:
+                m_tr(q_prev)
+            if r is not None:
+                r_tr(r, 0)
+                r_tr(r, 1)
+            if u_prev is not None:
+                p_tr(u_prev)
+            if q is not None:
+                m_cp(2 * q)
+                m_cp(2 * q + 1)
+            if q_prev is not None:
+                m_cp2(q_prev)
+                if q_prev % 4 == 3:
+                    later.setdefault(i + 2, []).append(("m", q_prev // 4))
+            if r is not None:
+                r_cp(r, 0)
+                r_cp(r, 1)
+            if u_prev is not None:
+                p_cp(u_prev)
+                if u_prev % 8 == 7:
+                    later.setdefault(i + 2, []).append(("p", u_prev // 8))
+            if r is not None:
+                r_tr(r, 2)
+                r_tr(r, 3)
+            grp = w_at.get(i)
+            if grp is not None:
+                w_tr(grp, 0)
+                w_tr(grp, 1)
+                if loads and grp not in (8, 9):
+                    w_load(loads.pop(0))
+            if i in p_at:
+                p_mul(p_at[i])
+            if r is not None:
+                r_cp(r, 2)
+                r_cp(r, 3)
+                later.setdefault(i + 3, []).append(("k", r))
+            if grp is not None:
+                w_cp(grp, 0)
+                w_cp(grp, 1)
+                later.setdefault(i + 3, []).append(("w", grp))
+            if acc_done == [acc_total, acc_total] and not turned:
+                turned.extend([out0_turn(0), out0_turn(1)])
+                out0_store(0, turned[0])
+                out0_store(1, turned[1])

import math
from contextlib import ExitStack

import concourse.mybir as mybir
from concourse.masks import make_identity

F32 = mybir.dt.float32
BF16 = mybir.dt.bfloat16
U32 = mybir.dt.uint32
U8 = mybir.dt.uint8
E4 = mybir.dt.float8_e4m3fn_x4
E5 = mybir.dt.float8_e5m2_x4
MULT = mybir.AluOpType.mult
ADD = mybir.AluOpType.add
COPY = mybir.ActivationFunctionType.Copy

P = 128
N, V = 1024, 128
FLOPS = 2 * N * V * (128 * 128 + 64 * 64 + 32 * 32) + 2 * N * V * 128 * 128
ALPHA0 = 1.0 / 128
ALPHA1 = 1.0 / math.sqrt(64 * 128)
ALPHA2 = 1.0 / 64
ROW = 144
DIRECT = 20
ROUTED = 32 - DIRECT


def tile_selfconnectionintro_v_kernel(tc, x, z, w0, w1, w2, grad_out, out_0, out_1):
    nc = tc.nc
    with ExitStack() as ctx:
        keep = ctx.enter_context(tc.tile_pool(name="keep", bufs=1))
        ring = ctx.enter_context(tc.tile_pool(name="ring", bufs=2))
        accp = ctx.enter_context(tc.psum_pool(name="accp", bufs=1))
        psum = ctx.enter_context(tc.psum_pool(name="psum", bufs=6))
        ctx.enter_context(tc.manual_schedule())

        def big(shape, dtype, name):
            t = ring.tile(shape, dtype, name=name, tag="big", bufs=5, align_bytes=64)
            return t

        def bank(name):
            t = psum.tile([P, 512], F32, name=name, tag="bank")
            return t

        x_v = x.rearrange("(g p j) w -> g p j w", g=2, j=4)
        g_v = grad_out.rearrange("(g p j) w -> g p j w", g=2, j=4)
        park_x = out_0[0 : 32 * DIRECT, :]
        park_m = out_1[92:128].rearrange("u v c -> (u v c)")

        first = ring.tile([P, 3, 2, 4, 128], BF16, name="first", tag="pp")
        g0, x0, zin = first[:, 0], first[:, 1], first[:, 2]
        for g in range(2):
            nc.sync.dma_start(out=g0[:, g], in_=g_v[g, :, :, 0:128])
            nc.sync.dma_start(out=x0[:, g], in_=x_v[g, :, :, 0:128])
        xr = ring.tile([P, 2, 4, 352], BF16, name="xr", tag="fm", align_bytes=64)
        gr = ring.tile([P, 2, 4, 352], BF16, name="gr", tag="fm", align_bytes=64)
        for g in range(2):
            nc.sync.dma_start(out=xr[:, g], in_=x_v[g, :, :, 128:480])
            nc.sync.dma_start(out=gr[:, g], in_=g_v[g, :, :, 128:480])
        nc.sync.dma_start(out=zin.rearrange("p g j v -> p g (j v)"), in_=z.rearrange("(g p j) v -> p g (j v)", g=2, j=4))

        ident = keep.tile([P, P], F32, name="ident")
        make_identity(nc, ident[:])
        pm = []
        for g in range(2):
            t = ring.tile([P, 4, 8, ROW], BF16, name="pm", tag="lhs")
            nc.gpsimd.memset(t[:].rearrange("p j r w -> p (j r w)").bitcast(F32), 0.0)
            pm.append(t)
        dts = []
        for i in range(4):
            t = keep.tile([P, 2, 256], BF16, name="dstage%d" % i)
            nc.gpsimd.memset(t[:, :, 224:256], 0.0)
            dts.append(t)

        w_raw, w_bank, w_t, w_codes, w_scales = {}, {}, {}, {}, {}

        def w_passes(grp):
            return 3 if grp == 10 else 4

        def w_load(grp):
            if grp < 8:
                t = ring.tile([P, 16, 128], BF16, name="wraw", tag="wraw")
                nc.sync.dma_start(out=t[:], in_=w0[16 * grp : 16 * grp + 16].rearrange("u v c -> v u c"))
                w_raw[grp] = t[:].rearrange("p u c -> p (u c)").bitcast(F32)
            elif grp == 8:
                t = big([P, 8, 512], BF16, "w_mix")
                nc.vector.memset(t[:, :, 448:512], 0.0)
                for a in range(5):
                    nc.sync.dma_start(out=t[:, :, 64 * a : 64 * a + 64], in_=w1[8 * a : 8 * a + 8].rearrange("u v c -> v u c"))
                for a in range(4):
                    nc.sync.dma_start(out=t[:, :, 320 + 32 * a : 352 + 32 * a], in_=w2[8 * a : 8 * a + 8].rearrange("u v c -> v u c"))
                for i in range(2):
                    w_raw[8 + i] = t[:, 4 * i : 4 * i + 4].rearrange("p u c -> p (u c)").bitcast(F32)
            elif grp == 10:
                t = ring.tile([P, 24, 64], BF16, name="wraw", tag="wraw")
                nc.sync.dma_start(out=t[:], in_=w1[40:64].rearrange("u v c -> v u c"))
                w_raw[grp] = t[:].rearrange("p u c -> p (u c)").bitcast(F32)

        def w_tr(grp, half):
            b = bank("wbank")
            for i in range(min(2, w_passes(grp) - 2 * half)):
                s = 2 * half + i
                for h in range(2):
                    nc.tensor.transpose(b[:, 256 * i + 128 * h : 256 * i + 128 * h + 128], w_raw[grp][:, 256 * s + h : 256 * s + 256 : 2], ident[:])
            w_bank[grp, half] = b

        def w_cp(grp, half):
            if half == 0:
                w_t[grp] = ring.tile([P, 4, 128, 2], F32, name="wt", tag="wt", align_bytes=64)
            n = min(2, w_passes(grp) - 2 * half)
            nc.scalar.copy(out=w_t[grp][:, 2 * half : 2 * half + n], in_=w_bank[grp, half][:, 0 : 256 * n].rearrange("p (s h v) -> p s v h", h=2, v=128))

        def w_q(grp):
            n = w_passes(grp)
            w_codes[grp] = keep.tile([P, 128 * n], U32, name="wc%d" % grp, align_bytes=64)
            w_scales[grp] = keep.tile([P, 128 * n], U8, name="ws%d" % grp, align_bytes=64)
            nc.vector.quantize_mx(out=w_codes[grp][:].bitcast(E4), scales=w_scales[grp][:], in_=w_t[grp][:, 0:n].rearrange("p s v h -> p (s v h)").bitcast(BF16))

        g0s = keep.tile([P, 2, 4, 128], BF16, name="g0s")
        g_tok = keep.tile([P, 8, 128], BF16, name="g_tok")
        x_tok = keep.tile([P, 32, 2, 64], BF16, name="x_tok")
        z_il = keep.tile([P, 2, 128, 4], BF16, name="z_il", align_bytes=64)
        z_codes = keep.tile([P, 256], U32, name="z_codes", align_bytes=64)
        z_scales = keep.tile([P, 256], U8, name="z_scales", align_bytes=64)

        x_il = keep.tile([P, 2, 128, 4], BF16, name="x_il")

        t_vals, t_codes, t_bank = {}, {}, {}

        def codes_tile():
            c = ring.tile([P, 1024], U32, name="codes", tag="codes", bufs=4, align_bytes=64)
            s = ring.tile([P, 1024], U8, name="scales", tag="scales", bufs=4, align_bytes=64)
            return c, s

        def quantize(vals):
            c, s = codes_tile()
            nc.vector.quantize_mx(out=c[:].bitcast(E5), scales=s[:], in_=vals)
            return c, s

        def t_gen(k):
            t = big([P, 4096], BF16, "tvals")
            nc.vector.tensor_tensor(
                out=t[:].rearrange("p (a u c j) -> p a u c j", a=8, u=4, j=4),
                in0=g_tok[:].rearrange("p a (c j) -> p a c j", j=4).unsqueeze(2).to_broadcast([P, 8, 4, 32, 4]),
                in1=x_tok[:, k].rearrange("p g (s u j) -> p (g s) u j", s=4, u=4).unsqueeze(3).to_broadcast([P, 8, 4, 32, 4]),
                op=MULT,
            )
            t_vals[k] = t

        def t_q(k):
            t_codes[k] = quantize(t_vals[k][:])

        def t_mm(k):
            b = bank("o1bank")
            c, s = t_codes[k]
            for g in range(2):
                nc.tensor.matmul_mx(
                    out=b[:],
                    lhsT=z_codes[:, 128 * g : 128 * g + 128].bitcast(E4),
                    lhsT_scale=z_scales[:, 128 * g : 128 * g + 128],
                    rhs=c[:, 512 * g : 512 * g + 512].bitcast(E5),
                    rhs_scale=s[:, 512 * g : 512 * g + 512],
                    start=(g == 0),
                    stop=(g == 1),
                )
            t_bank[k] = b

        def t_out(k):
            o = ring.tile([P, 4, 128], F32, name="o1", tag="ostage", bufs=3)
            nc.scalar.copy(out=o[:].rearrange("p u (c s) -> p (u c) s", s=4), in_=t_bank[k][:].rearrange("p (s q) -> p q s", s=4))
            nc.sync.dma_start(out=out_1[4 * k : 4 * k + 4].rearrange("u v c -> v u c"), in_=o[:])

        acc = [accp.tile([P, 512], F32, name="acc%d" % g) for g in range(2)]
        acc_done = [0, 0]
        acc_total = 32 + 3 + 4 * 8
        f_vals, f_codes = {}, {}

        def acc_mm(g, cols, grp, s, c, sc, c0):
            n = cols.stop - cols.start
            nc.tensor.matmul_mx(
                out=acc[g][:, cols],
                lhsT=w_codes[grp][:, 128 * s : 128 * s + 128].bitcast(E4),
                lhsT_scale=w_scales[grp][:, 128 * s : 128 * s + 128],
                rhs=c[:, c0 : c0 + n].bitcast(E5),
                rhs_scale=sc[:, c0 : c0 + n],
                start=(acc_done[g] == 0),
                stop=(acc_done[g] == acc_total - 1),
            )
            acc_done[g] = acc_done[g] + 1

        def f_q(key):
            f_codes[key] = quantize(f_vals[key][:])

        def f_mm(key):
            c, sc = f_codes[key]
            kind, i = key
            if kind == "m":
                for ug in range(8):
                    acc_mm(i // 4, slice(128 * (i % 4), 128 * (i % 4) + 128), 8 + ug // 4, ug % 4, c, sc, 128 * ug)
            else:
                grp, s = (10, i) if kind == "p" else (i // 4, i % 4)
                for g in range(2):
                    acc_mm(g, slice(0, 512), grp, s, c, sc, 512 * g)

        r_bank = {}

        def r_tr(k, q):
            g, h = q // 2, q % 2
            b = bank("rbank")
            words = t_vals[k][:].bitcast(F32)
            for s in range(4):
                c0 = 1024 * g + 256 * s
                nc.tensor.transpose(b[:, 128 * s : 128 * s + 128], words[:, c0 + h : c0 + 256 : 2], ident[:])
            r_bank[k, q] = b

        def r_cp(k, q):
            if q == 0:
                f_vals["k", k] = big([P, 4096], BF16, "fvals")
            nc.scalar.copy(
                out=f_vals["k", k][:, 1024 * q : 1024 * q + 1024].rearrange("p (e n s) -> p e n s", e=2, s=4),
                in_=r_bank[k, q][:].bitcast(BF16).rearrange("p (s n e) -> p e n s", s=4, e=2),
            )

        g_feat = keep.tile([P, 1024, 2], F32, name="g_feat")
        x_rows = {}

        def d_load(kd):
            t = ring.tile([P, 8, 128], F32, name="xrows", tag="xrows", bufs=3)
            src = park_x.rearrange("(t u k) n -> u k t n", t=8, u=4)
            for u in range(4):
                nc.sync.dma_start(out=t[32 * u : 32 * u + 32], in_=src[u, kd].unsqueeze(0).to_broadcast([32, 8, 128]))
            x_rows[kd] = t

        def d_gen(kd):
            t = big([P, 4096], BF16, "fvals")
            nc.vector.tensor_tensor(
                out=t[:].rearrange("p (n h e) -> p n h e", h=2, e=2),
                in0=g_feat[:].rearrange("p n h -> p (n h)").bitcast(BF16).rearrange("p (n h e) -> p n h e", h=2, e=2),
                in1=x_rows[kd][:].rearrange("p t n -> p (t n)").bitcast(BF16).rearrange("p (n e) -> p n e", e=2).unsqueeze(2).to_broadcast([P, 1024, 2, 2]),
                op=MULT,
            )
            f_vals["k", ROUTED + kd] = t

        mask = keep.tile([P, 16], F32, name="mask")
        xg = [keep.tile([P, 16, ROW // 2], F32, name="xg%d" % q) for q in range(4)]
        lhs, m_bank, m_bank2 = {}, {}, {}

        def l_build(c, n0, n1):
            if n0 == 0:
                lhs[c] = ring.tile([P, 8, 5, 16, 8], BF16, name="lhs", tag="lhs")
            src = xg[c // 2][:, 8 * (c % 2) : 8 * (c % 2) + 8].bitcast(BF16)[:, :, 0:40].rearrange("p g (a u) -> p g a u", u=8)
            for n in range(n0, n1):
                nc.vector.tensor_scalar(out=lhs[c][:, :, :, n, :], in0=src, scalar1=mask[:, n : n + 1], scalar2=None, op0=MULT)

        def m_mm(grp):
            b = bank("mbank")
            rhs = xg[grp // 16][:, grp % 16].bitcast(BF16)
            for a in range(5):
                n = 96 if a < 4 else 64
                nc.tensor.matmul(b[:, 96 * a : 96 * a + n], lhsT=lhs[grp // 8][:, grp % 8, a].rearrange("p n u -> p (n u)"), rhs=rhs[:, 48 : 48 + n], start=True, stop=True)
            m_bank[grp] = b

        def m_cp(grp):
            b, d = m_bank[grp], dts[grp % 4]
            sums = b[:, 0:480].rearrange("p (a w) -> p a w", w=96)
            nc.scalar.activation(
                out=d[:, :, 0:160].rearrange("p h (a w) -> p h a w", w=32),
                in_=sums[:, :, 0:64].rearrange("p a (h w) -> p h a w", h=2),
                func=COPY,
                scale=ALPHA1,
            )
            nc.scalar.activation(
                out=d[:, :, 160:224].rearrange("p h (a w) -> p h a w", w=16),
                in_=sums[:, 0:4, 64:96].rearrange("p a (h w) -> p h a w", h=2),
                func=COPY,
                scale=ALPHA2,
            )

        def m_tr(pair):
            b = bank("mbank2")
            for i in range(2):
                words = dts[(2 * pair + i) % 4][:].bitcast(F32)
                for h in range(2):
                    nc.tensor.transpose(b[:, 256 * h + 128 * i : 256 * h + 128 * i + 128], words[:, h], ident[:])
            m_bank2[pair] = b

        def m_cp2(pair):
            c = pair // 4
            if pair % 4 == 0:
                f_vals["m", c] = ring.tile([P, 4096], BF16, name="fm", tag="fm", align_bytes=64)
            dst = f_vals["m", c][:].bitcast(F32).rearrange("p (u n h) -> p u n h", u=8, h=2)
            nc.scalar.copy(out=dst[:, :, 32 * (pair % 4) : 32 * (pair % 4) + 32], in_=m_bank2[pair][:].rearrange("p (h n u) -> p u n h", h=2, u=8))

        g_p = keep.tile([P, 8, 3, 64], BF16, name="g_p")
        x_p = keep.tile([P, 8, 72], F32, name="x_p")
        prods, p_bank = {}, {}

        def p_mul(unit):
            s, t = unit // 8, unit % 8
            pp = ring.tile([P, 3, 4, 8, 16], F32, name="pp", tag="pp")
            for m in range(3):
                for u in range(8):
                    col = 3 * (8 * s + u) + m
                    nc.scalar.activation(out=pp[:, m, :, u, :], in_=g_p[:, t, m].rearrange("p (s c) -> p s c", s=4), func=COPY, scale=x_p[:, t, col : col + 1])
            prods[unit] = pp

        def p_tr(unit):
            b = bank("pbank")
            for s in range(4):
                for m in range(3):
                    nc.tensor.matmul(b[:, 128 * s : 128 * s + 128], lhsT=prods[unit][:, m, s].rearrange("p u c -> p (u c)"), rhs=ident[:], start=(m == 0), stop=(m == 2), is_transpose=True)
            p_bank[unit] = b

        def p_cp(unit):
            s, t = unit // 8, unit % 8
            if t == 0:
                f_vals["p", s] = ring.tile([P, 4096], BF16, name="fp", tag="fp", align_bytes=64)
            nc.scalar.activation(
                out=f_vals["p", s][:, 512 * t : 512 * t + 512].rearrange("p (n s) -> p n s", s=4),
                in_=p_bank[unit][:].rearrange("p (s n) -> p n s", s=4),
                func=COPY,
                scale=ALPHA1,
            )

        def x_park():
            x_dup = big([P, 8, 4, DIRECT, 2], BF16, "x_dup")
            src = x0[:, :, :, 4 * ROUTED : 128].rearrange("p g j (k u) -> p (g j) u k", u=4).unsqueeze(4).to_broadcast([P, 8, 4, DIRECT, 2])
            nc.scalar.copy(out=x_dup[:], in_=src)
            words = x_dup[:].rearrange("p t u k e -> p (t u k e)").bitcast(F32)
            blocks = DIRECT // 4
            for i0 in range(0, blocks, 4):
                n = min(4, blocks - i0)
                b = bank("xbank")
                for i in range(n):
                    nc.tensor.transpose(b[:, 128 * i : 128 * i + 128], words[:, 128 * (i0 + i) : 128 * (i0 + i) + 128], ident[:])
                x_t = ring.tile([P, 512], F32, name="x_t", tag="ostage", bufs=3)
                nc.scalar.copy(out=x_t[:, 0 : 128 * n], in_=b[:, 0 : 128 * n])
                nc.sync.dma_start(out=park_x[128 * i0 : 128 * (i0 + n)].rearrange("(i p) n -> p i n", p=P), in_=x_t[:, 0 : 128 * n].rearrange("p (i n) -> p i n", n=128))

        def m_park(g):
            t = pm[g]
            nc.scalar.copy(out=t[:, :, 0:3, 0:40], in_=xr[:, g, :, 0:120].rearrange("p j (u r) -> p j r u", r=3))
            nc.scalar.copy(out=t[:, :, 3:8, 0:32], in_=xr[:, g, :, 192:352].rearrange("p j (u r) -> p j r u", r=5))
            for h in range(2):
                nc.scalar.copy(
                    out=t[:, :, 0:3, 48 + 32 * h : 80 + 32 * h].rearrange("p j r (c e) -> p j r c e", e=2),
                    in_=gr[:, g, :, 0:192].rearrange("p j (c h e r) -> p h j r c e", h=2, e=2, r=3)[:, h],
                )
                nc.scalar.copy(
                    out=t[:, :, 3:8, 112 + 16 * h : 128 + 16 * h].rearrange("p j r (c e) -> p j r c e", e=2),
                    in_=gr[:, g, :, 192:352].rearrange("p j (c h e r) -> p h j r c e", h=2, e=2, r=5)[:, h],
                )
            nc.sync.dma_start(out=park_m.rearrange("(g j p w) -> g p j w", g=2, j=4, p=P)[g], in_=t[:].rearrange("p j r w -> p j (r w)").bitcast(F32))

        def xg_load(q):
            nc.sync.dma_start(out=xg[q][:], in_=park_m.rearrange("(g k w) -> k g w", k=P, w=ROW // 2)[:, 16 * q : 16 * q + 16])

        def t_fill():
            nc.vector.tensor_scalar(out=g0s[:].rearrange("p g j c -> p (g j c)"), in0=g0.rearrange("p g j c -> p (g j c)"), scalar1=ALPHA0, scalar2=None, op0=MULT)
            nc.vector.tensor_copy(out=x_il[:], in_=x0.rearrange("p g j u -> p g u j"))
            nc.vector.tensor_copy(out=g_tok[:].rearrange("p (g s) (c j) -> p g s c j", g=2, j=4), in_=g0s[:].rearrange("p g j (c s) -> p g s c j", s=4))
            for g in range(2):
                src = x_il[:, g].rearrange("p (k u) j -> p k (u j)", u=4).unsqueeze(2).to_broadcast([P, 32, 4, 16])
                nc.vector.tensor_copy(out=x_tok[:, :, g].rearrange("p k (s q) -> p k s q", s=4), in_=src)

        def z_fill():
            nc.vector.tensor_copy(out=z_il[:], in_=zin.rearrange("p g j v -> p g v j"))
            nc.vector.tensor_reduce(out=mask[:], in_=ident[:].rearrange("p (n r) -> p n r", r=8), axis=mybir.AxisListType.X, op=ADD)
            nc.vector.quantize_mx(out=z_codes[:].bitcast(E4), scales=z_scales[:], in_=z_il[:].rearrange("p g v j -> p (g v j)"))

        def g_feat_fill():
            g_rep = big([P, 8, 2, 128], F32, "g_rep")
            src = g0s[:].rearrange("p g j c -> p (g j) c").bitcast(F32).rearrange("p t (c h) -> p t h c", h=2).unsqueeze(3).to_broadcast([P, 8, 2, 4, 32])
            nc.scalar.copy(out=g_rep[:].rearrange("p t h (u c) -> p t h u c", u=4), in_=src)
            for q in range(4):
                b = bank("gbank")
                for i in range(4):
                    nc.tensor.transpose(b[:, 128 * i : 128 * i + 128], g_rep[:, 2 * q + i // 2, i % 2], ident[:])
                nc.scalar.copy(out=g_feat[:, 256 * q : 256 * q + 256].rearrange("p (t n) h -> p t n h", t=2), in_=b[:].rearrange("p (t h n) -> p t n h", t=2, h=2))

        def p_fill():
            nc.scalar.copy(out=g_p[:].rearrange("p t m (s c) -> p t m s c", s=4), in_=gr[:, :, :, 0:192].rearrange("p g j (c s m) -> p (g j) m s c", s=4, m=3))
            nc.scalar.copy(out=x_p[:], in_=xr[:, :, :, 120:192].rearrange("p g j w -> p (g j) w"))

        def out0_turn(g):
            a_sb = ring.tile([P, 512], F32, name="a_sb", tag="pp")
            nc.scalar.copy(out=a_sb[:], in_=acc[g][:])
            b = bank("obank")
            for j in range(4):
                nc.tensor.transpose(b[:, 128 * j : 128 * j + 128], a_sb[:, 128 * j : 128 * j + 128], ident[:])
            return b

        def out0_store(g, b):
            o = ring.tile([P, 512], F32, name="o0", tag="xrows", bufs=3)
            nc.scalar.copy(out=o[:], in_=b[:])
            nc.sync.dma_start(out=out_0.rearrange("(g p j) v -> g p (j v)", g=2, j=4)[g], in_=o[:])

        first_t, last_t = 3, 2
        mid = 32 - first_t - last_t
        units = [("t", None)] * first_t
        for i in range(DIRECT):
            units.append(("d", i))
            units.extend([("t", None)] * ((i + 1) * mid // DIRECT - i * mid // DIRECT))
        units.extend([("t", None)] * last_t)
        t_slots = [i for i, u in enumerate(units) if u[0] == "t"]
        inner = t_slots[first_t : 32 - last_t - 2]
        routed_slots = [inner[(2 * r + 1) * len(inner) // (2 * ROUTED)] for r in range(ROUTED)]
        plain_k = list(range(ROUTED, 32))
        for i in t_slots:
            units[i] = ("t", routed_slots.index(i) if i in routed_slots else plain_k.pop(0))
        slots = len(units)
        m0, m1 = 8, slots - 4
        m_at = {m0 + q * (m1 - m0) // 32: q for q in range(32)}
        free = [i for i in range(2, slots - 4) if i - 1 not in routed_slots]
        p_at = {free[u * len(free) // 24]: u for u in range(24)}
        need = {}
        for i, (kind, k) in enumerate(units):
            if kind == "d":
                need.setdefault((ROUTED + k) // 4, i + 1)
            elif k < ROUTED:
                need.setdefault(k // 4, i + 4)
        need[8], need[9], need[10] = m0 + 6, m0 + 7, m0 + 8
        w_at = {}
        for grp in sorted(need, key=lambda q: -need[q]):
            i = need[grp] - 4
            while i in w_at or i + 1 in w_at:
                i = i - 1
            w_at[i] = grp
        w_order = [w_at[i] for i in sorted(w_at)]
        loads = [grp for grp in w_order if grp != 9]
        w_load(loads[0])
        t_fill()
        x_park()
        d_load(0)
        g_feat_fill()
        p_fill()
        d_load(1)
        loads = [grp for grp in loads[1:] if grp != 8]
        w_load(loads.pop(0))

        made, quantized, later, turned = [], [], {}, []
        for i in range(slots + 2):
            kind, k = units[i] if i < slots else (None, None)
            if kind == "t":
                t_gen(k)
            if kind == "d":
                d_gen(k)
                if k + 2 < DIRECT:
                    d_load(k + 2)
            if i == 1:
                z_fill()
                m_park(0)
                xg_load(0)
            if i == 3:
                m_park(1)
            if i == m0 - 4:
                w_load(8)
            if m_at.get(i) in (0, 6, 14):
                xg_load((m_at[i] + 10) // 8)
            done = quantized
            quantized = []
            for key in done:
                if key[0] == "t":
                    t_mm(key[1])
                else:
                    f_mm(key)
            q = m_at.get(i)
            if q is not None:
                m_mm(2 * q)
                m_mm(2 * q + 1)
            for key in made + later.get(i, []):
                if key[0] == "t":
                    t_q(key[1])
                    quantized.append(key)
                elif key[0] == "w":
                    w_q(key[1])
                else:
                    f_q(key)
                    quantized.append(key)
            made = [("t", k) if kind == "t" else ("k", ROUTED + k)] if i < slots else []
            for lead in (1, 2):
                c = m_at.get(i + lead)
                if c is not None and c % 4 == 0:
                    l_build(c // 4, 16 - 8 * lead, 24 - 8 * lead)
            r = units[i - 1][1] if i - 1 in routed_slots else None
            u_prev = p_at.get(i - 1)
            for key in done:
                if key[0] == "t":
                    t_out(key[1])
            q_prev = m_at.get(i - 1)
            if q_prev is not None:
                m_tr(q_prev)
            if r is not None:
                r_tr(r, 0)
                r_tr(r, 1)
            if u_prev is not None:
                p_tr(u_prev)
            if q is not None:
                m_cp(2 * q)
                m_cp(2 * q + 1)
            if q_prev is not None:
                m_cp2(q_prev)
                if q_prev % 4 == 3:
                    later.setdefault(i + 2, []).append(("m", q_prev // 4))
            if r is not None:
                r_cp(r, 0)
                r_cp(r, 1)
            if u_prev is not None:
                p_cp(u_prev)
                if u_prev % 8 == 7:
                    later.setdefault(i + 2, []).append(("p", u_prev // 8))
            if r is not None:
                r_tr(r, 2)
                r_tr(r, 3)
            grp = w_at.get(i)
            if grp is not None:
                w_tr(grp, 0)
                w_tr(grp, 1)
                if loads and grp not in (8, 9):
                    w_load(loads.pop(0))
            if i in p_at:
                p_mul(p_at[i])
            if r is not None:
                r_cp(r, 2)
                r_cp(r, 3)
                later.setdefault(i + 3, []).append(("k", r))
            if grp is not None:
                w_cp(grp, 0)
                w_cp(grp, 1)
                later.setdefault(i + 3, []).append(("w", grp))
            if acc_done == [acc_total, acc_total] and not turned:
                turned.extend([out0_turn(0), out0_turn(1)])
                out0_store(0, turned[0])
                out0_store(1, turned[1])
